import numpy as np
import ml_dtypes


def mxq(x, axis, fmt="e4m3"):
    dtype, down = {"e4m3": (ml_dtypes.float8_e4m3fn, 7), "e5m2": (ml_dtypes.float8_e5m2, 14)}[fmt]
    v = np.moveaxis(np.asarray(x, np.float32).astype(ml_dtypes.bfloat16).astype(np.float64), axis, -1)
    blocks = v.reshape(v.shape[:-1] + (-1, 32))
    amax = np.abs(blocks).max(-1, keepdims=True)
    byte = np.maximum(np.where(amax > 0, np.frexp(amax)[1] - 1 + 127, 0) - down, 1)
    scale = np.exp2(byte - 127.0)
    codes = (blocks / scale).astype(np.float32).astype(dtype).astype(np.float64)
    return np.moveaxis((codes * scale).reshape(v.shape), -1, axis)


WIDE = False


def mx_kscale(k):
    if not WIDE:
        return np.ones(k)
    levels = np.array([10, -10, 5, -5, 0])
    if k % 512:
        return np.exp2(np.random.permutation(np.resize(levels, k // 32))).repeat(32)
    a = np.empty((k // 512, 16))
    for p in range(k // 512):
        a[p, :8] = np.random.permutation(np.resize(levels, 8))
        for g in range(8):
            far = levels[np.abs(levels - a[p, g]) >= 10]
            a[p, g + 8] = far[np.random.randint(len(far))]
    return np.exp2(a.ravel()).repeat(32)


BF16 = ml_dtypes.bfloat16


def bf(x):
    return np.asarray(x, np.float32).astype(BF16)


def f64(x):
    return np.asarray(x).astype(np.float64)


B, L, LQ, DM, DH, W = 2, 8192, 1024, 512, 128, 512
C = L // W


def chunk_banks(x):
    z = np.zeros_like(x[:, :1])
    prev = np.concatenate((z, x[:, :-1]), axis=1)
    nxt = np.concatenate((x[:, 1:], z), axis=1)
    return np.stack((prev, x, nxt), axis=1).sum(axis=2)


def setup_inputs():
    s = mx_kscale(DM)
    return {"kv": bf(np.random.standard_normal((B, L, DM)) * s),
            "Wkv": bf(np.random.standard_normal((DM, 2 * DH)) * 2.0 / np.sqrt(DM * C) / s[:, None])}


def reference(kv, Wkv):
    kvp = mxq(f64(kv), 2, "e4m3") @ mxq(f64(Wkv), 0, "e4m3")
    k, v = kvp[..., :DH], kvp[..., DH:]
    return chunk_banks(k.reshape(B, C, W, DH)), v

@@ -1,0 +1,212 @@
+from contextlib import ExitStack
+
+import concourse.mybir as mybir
+from concourse.masks import make_identity
+
+F32 = mybir.dt.float32
+BF16 = mybir.dt.bfloat16
+U32 = mybir.dt.uint32
+U8 = mybir.dt.uint8
+FP8X4 = mybir.dt.float8_e4m3fn_x4
+ADD = mybir.AluOpType.add
+
+P = 128
+PACK = 4
+BATCH, LENGTH, D_MODEL, D_HEAD, CHUNK = 2, 8192, 512, 128, 512
+N_STEPS = LENGTH // CHUNK
+EDGES = 2
+ROWS = BATCH * CHUNK
+TILES = ROWS // P
+BANK = 512
+HALVES = ROWS // BANK
+TILES_PER_HALF = TILES // HALVES
+WORDS = D_MODEL // 2
+ALL_BUT_LAST, ALL, ALL_BUT_FIRST = 0, 1, 2
+KV_BUFS = N_STEPS // 2
+V_ON_SCALAR_FROM = N_STEPS - 2
+
+FLOPS = 2 * BATCH * LENGTH * D_MODEL * 2 * D_HEAD
+
+
+def chunk_of_step(s):
+    return (0, N_STEPS - 1)[s] if s < EDGES else s - 1
+
+
+def tile_localxlattention_pa_t_kernel(tc, kv, Wkv, k_ext, v):
+    nc = tc.nc
+    with ExitStack() as ctx:
+        ctx.enter_context(tc.manual_schedule())
+        const = ctx.enter_context(tc.tile_pool(name="const", bufs=1))
+        kv_pool = ctx.enter_context(tc.tile_pool(name="kv", bufs=KV_BUFS))
+        mx_pool = ctx.enter_context(tc.tile_pool(name="mx", bufs=2))
+        v_pool = ctx.enter_context(tc.tile_pool(name="v", bufs=N_STEPS))
+        turn_psum = ctx.enter_context(tc.psum_pool(name="turn", bufs=4))
+        v_psum = ctx.enter_context(tc.psum_pool(name="vp", bufs=HALVES))
+        k_psum = ctx.enter_context(tc.psum_pool(name="kp", bufs=HALVES))
+
+        kv_tiles = {}
+        quantised = {}
+        v_tiles = {}
+        k_open = {}
+
+        def chunk_rows(dram, s, b):
+            first = chunk_of_step(s) * CHUNK
+            return dram[b, first : first + CHUNK, :].rearrange("(q t) d -> q (t d)", t=TILES)
+
+        def load(s):
+            x = kv_pool.tile([P, TILES * D_MODEL], BF16, name="x")
+            for b in range(BATCH):
+                nc.sync.dma_start(out=x[b:P:BATCH, :], in_=chunk_rows(kv, s, b))
+            kv_tiles[s] = x
+
+        def transpose_and_regroup(s):
+            words = kv_tiles[s][:].bitcast(F32)
+            grouped = mx_pool.tile([P, ROWS * PACK], BF16, name="grouped", align_bytes=64)
+            grouped_words = grouped[:].bitcast(F32).rearrange("w (n u) -> w n u", u=2)
+            for pair in range(TILES // 2):
+                turned = turn_psum.tile([P, BANK], F32, name="turned")
+                by_u = turned[:].rearrange("w (u n) -> w u n", u=2)
+                for i in range(2):
+                    t = 2 * pair + i
+                    for u in range(2):
+                        nc.tensor.transpose(
+                            by_u[:, u, i * P : (i + 1) * P],
+                            words[:, t * WORDS + u : (t + 1) * WORDS : 2],
+                            ident[:],
+                        )
+                nc.scalar.copy(
+                    out=grouped_words[:, 2 * pair * P : 2 * (pair + 1) * P, :],
+                    in_=by_u.rearrange("w u n -> w n u"),
+                )
+            codes = mx_pool.tile([P, ROWS], U32, name="codes", align_bytes=64)
+            scales = mx_pool.tile([P, ROWS], U8, name="scales", align_bytes=64)
+            quantised[s] = (codes, scales)
+            return grouped
+
+        def quantise(s, h, grouped):
+            codes, scales = quantised[s]
+            cols = slice(h * BANK, (h + 1) * BANK)
+            nc.vector.quantize_mx(
+                out=codes[:, cols].bitcast(FP8X4),
+                scales=scales[:, cols],
+                in_=grouped[:, h * BANK * PACK : (h + 1) * BANK * PACK],
+            )
+
+        def multiply(s, h):
+            codes, scales = quantised[s]
+            cols = slice(h * BANK, (h + 1) * BANK)
+            start = s <= EDGES
+            stop = s < EDGES or s == N_STEPS - 1
+            if start:
+                k_open[h] = k_psum.tile([P, BANK], F32, name="k_acc")
+            nc.tensor.matmul_mx(
+                out=k_open[h][:],
+                lhsT=w_codes[:, 0:D_HEAD].bitcast(FP8X4),
+                lhsT_scale=w_scales[:, 0:D_HEAD],
+                rhs=codes[:, cols].bitcast(FP8X4),
+                rhs_scale=scales[:, cols],
+                start=start,
+                stop=stop,
+            )
+            v_acc = v_psum.tile([P, TILES_PER_HALF, D_HEAD], F32, name="v_acc")
+            for i in range(TILES_PER_HALF):
+                tile_cols = slice(h * BANK + i * P, h * BANK + (i + 1) * P)
+                nc.tensor.matmul_mx(
+                    out=v_acc[:, i, :],
+                    lhsT=codes[:, tile_cols].bitcast(FP8X4),
+                    lhsT_scale=scales[:, tile_cols],
+                    rhs=w_codes[:, D_HEAD : 2 * D_HEAD].bitcast(FP8X4),
+                    rhs_scale=w_scales[:, D_HEAD : 2 * D_HEAD],
+                    start=True,
+                    stop=True,
+                )
+            return v_acc
+
+        def copy_v_out(s, h, v_acc):
+            v_half = v_tiles[s][:, h * TILES_PER_HALF : (h + 1) * TILES_PER_HALF, :]
+            if s >= V_ON_SCALAR_FROM:
+                nc.scalar.copy(out=v_half, in_=v_acc[:])
+            else:
+                nc.vector.tensor_copy(out=v_half, in_=v_acc[:])
+
+        def turn_k_back(j, h):
+            turned = turn_psum.tile([P, BANK], F32, name="turned")
+            for i in range(TILES_PER_HALF):
+                nc.tensor.transpose(
+                    turned[:, i * D_HEAD : (i + 1) * D_HEAD],
+                    k_sumsT[:, j, h, i * P : (i + 1) * P],
+                    ident[:],
+                )
+            nc.scalar.copy(out=k_sums[:, j, h, :], in_=turned[:])
+
+        for s in range(KV_BUFS):
+            load(s)
+
+        ident = const.tile([P, P], F32, name="ident")
+        make_identity(nc, ident[:])
+
+        w_rows = const.tile([P, PACK, 2 * D_HEAD], BF16, name="w_rows")
+        nc.scalar.dma_start(out=w_rows[:], in_=Wkv.rearrange("(w j) n -> w j n", j=PACK))
+        w_grouped = const.tile([P, 2 * D_HEAD, PACK], BF16, name="w_grouped", align_bytes=64)
+        nc.vector.tensor_copy(out=w_grouped[:], in_=w_rows[:].rearrange("w j n -> w n j"))
+        w_codes = const.tile([P, 2 * D_HEAD], U32, name="w_codes", align_bytes=64)
+        w_scales = const.tile([P, 2 * D_HEAD], U8, name="w_scales", align_bytes=64)
+        nc.vector.quantize_mx(
+            out=w_codes[:].bitcast(FP8X4),
+            scales=w_scales[:],
+            in_=w_grouped[:].rearrange("w n j -> w (n j)"),
+        )
+
+        k_edge = const.tile([P, EDGES, HALVES, BANK], F32, name="k_edge")
+        k_sumsT = const.tile([P, 3, HALVES, BANK], F32, name="k_sumsT")
+        k_sums = const.tile([P, 3, HALVES, BANK], F32, name="k_sums")
+
+        for r in range(N_STEPS + 1):
+            if r < N_STEPS:
+                grouped = transpose_and_regroup(r)
+                if r + KV_BUFS < N_STEPS:
+                    load(r + KV_BUFS)
+            if r >= 1:
+                v_tiles[r - 1] = v_pool.tile([P, TILES, D_HEAD], F32, name="v_sb")
+                v_accs = [multiply(r - 1, h) for h in range(HALVES)]
+            for h in range(HALVES):
+                if r < N_STEPS:
+                    quantise(r, h, grouped)
+                if r >= 1:
+                    copy_v_out(r - 1, h, v_accs[h])
+            if 1 <= r <= EDGES:
+                for h in range(HALVES):
+                    nc.scalar.copy(out=k_edge[:, r - 1, h, :], in_=k_open[h][:])
+
+        for h in range(HALVES):
+            nc.vector.tensor_tensor(
+                out=k_sumsT[:, ALL_BUT_LAST, h, :], in0=k_open[h][:], in1=k_edge[:, 0, h, :], op=ADD
+            )
+        for h in range(HALVES):
+            nc.vector.tensor_tensor(
+                out=k_sumsT[:, ALL_BUT_FIRST, h, :], in0=k_open[h][:], in1=k_edge[:, 1, h, :], op=ADD
+            )
+        for h in range(HALVES):
+            nc.vector.tensor_tensor(
+                out=k_sumsT[:, ALL, h, :],
+                in0=k_sumsT[:, ALL_BUT_LAST, h, :],
+                in1=k_edge[:, 1, h, :],
+                op=ADD,
+            )
+        banks_as_summed = (ALL_BUT_LAST, ALL_BUT_FIRST, ALL)
+        for j in banks_as_summed:
+            for h in range(HALVES):
+                turn_k_back(j, h)
+
+        for s in range(N_STEPS):
+            for b in range(BATCH):
+                nc.sync.dma_start(
+                    out=chunk_rows(v, s, b),
+                    in_=v_tiles[s][b:P:BATCH, :, :].rearrange("q t d -> q (t d)"),
+                )
+        for j in banks_as_summed:
+            for b in range(BATCH):
+                nc.sync.dma_start(
+                    out=k_ext[b, j].rearrange("(q t) d -> q (t d)", t=TILES),
+                    in_=k_sums[b:P:BATCH, j, :, :].rearrange("q h n -> q (h n)"),
+                )

@@ -20,7 +20,6 @@ TILES = ROWS // P
 BANK = 512
 HALVES = ROWS // BANK
 TILES_PER_HALF = TILES // HALVES
-WORDS = D_MODEL // 2
 ALL_BUT_LAST, ALL, ALL_BUT_FIRST = 0, 1, 2
 KV_BUFS = N_STEPS // 2
 V_ON_SCALAR_FROM = N_STEPS - 2
@@ -39,12 +38,14 @@ def tile_localxlattention_pa_t_kernel(tc, kv, Wkv, k_ext, v):
         const = ctx.enter_context(tc.tile_pool(name="const", bufs=1))
         kv_pool = ctx.enter_context(tc.tile_pool(name="kv", bufs=KV_BUFS))
         mx_pool = ctx.enter_context(tc.tile_pool(name="mx", bufs=2))
+        split_pool = ctx.enter_context(tc.tile_pool(name="split", bufs=2))
         v_pool = ctx.enter_context(tc.tile_pool(name="v", bufs=N_STEPS))
         turn_psum = ctx.enter_context(tc.psum_pool(name="turn", bufs=4))
         v_psum = ctx.enter_context(tc.psum_pool(name="vp", bufs=HALVES))
         k_psum = ctx.enter_context(tc.psum_pool(name="kp", bufs=HALVES))
 
         kv_tiles = {}
+        split_tiles = {}
         quantised = {}
         v_tiles = {}
         k_open = {}
@@ -53,14 +54,24 @@ def tile_localxlattention_pa_t_kernel(tc, kv, Wkv, k_ext, v):
             first = chunk_of_step(s) * CHUNK
             return dram[b, first : first + CHUNK, :].rearrange("(q t) d -> q (t d)", t=TILES)
 
-        def load(s):
+        def load(s, pieces=1):
             x = kv_pool.tile([P, TILES * D_MODEL], BF16, name="x")
-            for b in range(BATCH):
-                nc.sync.dma_start(out=x[b:P:BATCH, :], in_=chunk_rows(kv, s, b))
+            width = TILES * D_MODEL // pieces
+            for i in range(pieces):
+                cols = slice(i * width, (i + 1) * width)
+                for b in range(BATCH):
+                    nc.sync.dma_start(out=x[b:P:BATCH, cols], in_=chunk_rows(kv, s, b)[:, cols])
             kv_tiles[s] = x
 
+        def split_words(s):
+            split = split_pool.tile([P, TILES, 2, P], F32, name="split")
+            words = kv_tiles[s][:].bitcast(F32).rearrange("p (t w u) -> p t u w", t=TILES, u=2)
+            for h in range(HALVES):
+                tiles = slice(h * TILES_PER_HALF, (h + 1) * TILES_PER_HALF)
+                nc.vector.tensor_copy(out=split[:, tiles, :, :], in_=words[:, tiles, :, :])
+            split_tiles[s] = split
+
         def transpose_and_regroup(s):
-            words = kv_tiles[s][:].bitcast(F32)
             grouped = mx_pool.tile([P, ROWS * PACK], BF16, name="grouped", align_bytes=64)
             grouped_words = grouped[:].bitcast(F32).rearrange("w (n u) -> w n u", u=2)
             for pair in range(TILES // 2):
@@ -71,7 +82,7 @@ def tile_localxlattention_pa_t_kernel(tc, kv, Wkv, k_ext, v):
                     for u in range(2):
                         nc.tensor.transpose(
                             by_u[:, u, i * P : (i + 1) * P],
-                            words[:, t * WORDS + u : (t + 1) * WORDS : 2],
+                            split_tiles[s][:, t, u, :],
                             ident[:],
                         )
                 nc.scalar.copy(
@@ -124,7 +135,7 @@ def tile_localxlattention_pa_t_kernel(tc, kv, Wkv, k_ext, v):
 
         def copy_v_out(s, h, v_acc):
             v_half = v_tiles[s][:, h * TILES_PER_HALF : (h + 1) * TILES_PER_HALF, :]
-            if s >= V_ON_SCALAR_FROM:
+            if h == 1 or s >= V_ON_SCALAR_FROM:
                 nc.scalar.copy(out=v_half, in_=v_acc[:])
             else:
                 nc.vector.tensor_copy(out=v_half, in_=v_acc[:])
@@ -140,13 +151,19 @@ def tile_localxlattention_pa_t_kernel(tc, kv, Wkv, k_ext, v):
             nc.scalar.copy(out=k_sums[:, j, h, :], in_=turned[:])
 
         for s in range(KV_BUFS):
-            load(s)
+            load(s, pieces=HALVES if s == 0 else 1)
 
         ident = const.tile([P, P], F32, name="ident")
         make_identity(nc, ident[:])
 
         w_rows = const.tile([P, PACK, 2 * D_HEAD], BF16, name="w_rows")
         nc.scalar.dma_start(out=w_rows[:], in_=Wkv.rearrange("(w j) n -> w j n", j=PACK))
+        k_edge = const.tile([P, EDGES, HALVES, BANK], F32, name="k_edge")
+        k_sumsT = const.tile([P, 3, HALVES, BANK], F32, name="k_sumsT")
+        k_sums = const.tile([P, 3, HALVES, BANK], F32, name="k_sums")
+
+        split_words(0)
+        load(KV_BUFS)
         w_grouped = const.tile([P, 2 * D_HEAD, PACK], BF16, name="w_grouped", align_bytes=64)
         nc.vector.tensor_copy(out=w_grouped[:], in_=w_rows[:].rearrange("w j n -> w n j"))
         w_codes = const.tile([P, 2 * D_HEAD], U32, name="w_codes", align_bytes=64)
@@ -157,15 +174,13 @@ def tile_localxlattention_pa_t_kernel(tc, kv, Wkv, k_ext, v):
             in_=w_grouped[:].rearrange("w n j -> w (n j)"),
         )
 
-        k_edge = const.tile([P, EDGES, HALVES, BANK], F32, name="k_edge")
-        k_sumsT = const.tile([P, 3, HALVES, BANK], F32, name="k_sumsT")
-        k_sums = const.tile([P, 3, HALVES, BANK], F32, name="k_sums")
-
         for r in range(N_STEPS + 1):
             if r < N_STEPS:
                 grouped = transpose_and_regroup(r)
-                if r + KV_BUFS < N_STEPS:
-                    load(r + KV_BUFS)
+            if r + 1 < N_STEPS:
+                split_words(r + 1)
+                if r + 1 + KV_BUFS < N_STEPS:
+                    load(r + 1 + KV_BUFS)
             if r >= 1:
                 v_tiles[r - 1] = v_pool.tile([P, TILES, D_HEAD], F32, name="v_sb")
                 v_accs = [multiply(r - 1, h) for h in range(HALVES)]

@@ -13,22 +13,30 @@ ADD = mybir.AluOpType.add
 P = 128
 PACK = 4
 BATCH, LENGTH, D_MODEL, D_HEAD, CHUNK = 2, 8192, 512, 128, 512
-N_STEPS = LENGTH // CHUNK
+CHUNKS = LENGTH // CHUNK
+TOTAL = BATCH * CHUNKS
 EDGES = 2
-ROWS = BATCH * CHUNK
-TILES = ROWS // P
+TILES = CHUNK // P
+PAIR = 2
+STEP = 2
+N_STEPS = TOTAL // STEP
+GROUP = 4
+N_GROUPS = TOTAL // GROUP
+KV_BUFS = N_GROUPS // 2
 BANK = 512
-HALVES = ROWS // BANK
-TILES_PER_HALF = TILES // HALVES
 ALL_BUT_LAST, ALL, ALL_BUT_FIRST = 0, 1, 2
-KV_BUFS = N_STEPS // 2
-V_ON_SCALAR_FROM = N_STEPS - 2
+BANKS_AS_SUMMED = (ALL_BUT_LAST, ALL_BUT_FIRST, ALL)
 
 FLOPS = 2 * BATCH * LENGTH * D_MODEL * 2 * D_HEAD
 
 
-def chunk_of_step(s):
-    return (0, N_STEPS - 1)[s] if s < EDGES else s - 1
+def item_of(g):
+    return g // CHUNKS
+
+
+def chunk_of(g):
+    i = g % CHUNKS
+    return (0, CHUNKS - 1)[i] if i < EDGES else i - 1
 
 
 def tile_localxlattention_pa_t_kernel(tc, kv, Wkv, k_ext, v):
@@ -37,95 +45,95 @@ def tile_localxlattention_pa_t_kernel(tc, kv, Wkv, k_ext, v):
         ctx.enter_context(tc.manual_schedule())
         const = ctx.enter_context(tc.tile_pool(name="const", bufs=1))
         kv_pool = ctx.enter_context(tc.tile_pool(name="kv", bufs=KV_BUFS))
-        mx_pool = ctx.enter_context(tc.tile_pool(name="mx", bufs=2))
-        split_pool = ctx.enter_context(tc.tile_pool(name="split", bufs=2))
-        v_pool = ctx.enter_context(tc.tile_pool(name="v", bufs=N_STEPS))
+        mx_pool = ctx.enter_context(tc.tile_pool(name="mx", bufs=2 * STEP))
+        v_pool = ctx.enter_context(tc.tile_pool(name="v", bufs=N_GROUPS))
         turn_psum = ctx.enter_context(tc.psum_pool(name="turn", bufs=4))
-        v_psum = ctx.enter_context(tc.psum_pool(name="vp", bufs=HALVES))
-        k_psum = ctx.enter_context(tc.psum_pool(name="kp", bufs=HALVES))
+        v_psum = ctx.enter_context(tc.psum_pool(name="vp", bufs=STEP))
+        k_psum = ctx.enter_context(tc.psum_pool(name="kp", bufs=EDGES))
 
         kv_tiles = {}
-        split_tiles = {}
-        quantised = {}
         v_tiles = {}
+        split_tiles = {}
+        grouped_tiles = {}
+        quantised = {}
         k_open = {}
 
-        def chunk_rows(dram, s, b):
-            first = chunk_of_step(s) * CHUNK
-            return dram[b, first : first + CHUNK, :].rearrange("(q t) d -> q (t d)", t=TILES)
+        def chunk_rows(dram, g, n):
+            by_chunk = dram[item_of(g)].rearrange("(c p t) d -> p c (t d)", p=P, t=TILES)
+            first = chunk_of(g)
+            stride = chunk_of(g + 1) - first if n > 1 else 1
+            return by_chunk[:, first : first + (n - 1) * stride + 1 : stride, :]
 
-        def load(s, pieces=1):
-            x = kv_pool.tile([P, TILES * D_MODEL], BF16, name="x")
-            width = TILES * D_MODEL // pieces
-            for i in range(pieces):
-                cols = slice(i * width, (i + 1) * width)
-                for b in range(BATCH):
-                    nc.sync.dma_start(out=x[b:P:BATCH, cols], in_=chunk_rows(kv, s, b)[:, cols])
-            kv_tiles[s] = x
+        def load(group, pieces):
+            x = kv_pool.tile([P, GROUP, TILES * D_MODEL], BF16, name="x")
+            at = 0
+            for n in pieces:
+                nc.sync.dma_start(
+                    out=x[:, at : at + n, :], in_=chunk_rows(kv, group * GROUP + at, n)
+                )
+                at += n
+            kv_tiles[group] = x
 
-        def split_words(s):
-            split = split_pool.tile([P, TILES, 2, P], F32, name="split")
-            words = kv_tiles[s][:].bitcast(F32).rearrange("p (t w u) -> p t u w", t=TILES, u=2)
-            for h in range(HALVES):
-                tiles = slice(h * TILES_PER_HALF, (h + 1) * TILES_PER_HALF)
-                nc.vector.tensor_copy(out=split[:, tiles, :, :], in_=words[:, tiles, :, :])
-            split_tiles[s] = split
+        def split_words(g):
+            split = mx_pool.tile([P, TILES, 2, P], F32, name="split")
+            words = kv_tiles[g // GROUP][:, g % GROUP, :].bitcast(F32)
+            nc.vector.tensor_copy(
+                out=split[:], in_=words.rearrange("p (t w u) -> p t u w", t=TILES, u=2)
+            )
+            split_tiles[g] = split
 
-        def transpose_and_regroup(s):
-            grouped = mx_pool.tile([P, ROWS * PACK], BF16, name="grouped", align_bytes=64)
+        def transpose_and_regroup(g):
+            grouped = mx_pool.tile([P, CHUNK * PACK], BF16, name="grouped", align_bytes=64)
             grouped_words = grouped[:].bitcast(F32).rearrange("w (n u) -> w n u", u=2)
-            for pair in range(TILES // 2):
+            for first in range(0, TILES, PAIR):
                 turned = turn_psum.tile([P, BANK], F32, name="turned")
                 by_u = turned[:].rearrange("w (u n) -> w u n", u=2)
-                for i in range(2):
-                    t = 2 * pair + i
+                for i in range(PAIR):
                     for u in range(2):
                         nc.tensor.transpose(
                             by_u[:, u, i * P : (i + 1) * P],
-                            split_tiles[s][:, t, u, :],
+                            split_tiles[g][:, first + i, u, :],
                             ident[:],
                         )
                 nc.scalar.copy(
-                    out=grouped_words[:, 2 * pair * P : 2 * (pair + 1) * P, :],
+                    out=grouped_words[:, first * P : (first + PAIR) * P, :],
                     in_=by_u.rearrange("w u n -> w n u"),
                 )
-            codes = mx_pool.tile([P, ROWS], U32, name="codes", align_bytes=64)
-            scales = mx_pool.tile([P, ROWS], U8, name="scales", align_bytes=64)
-            quantised[s] = (codes, scales)
-            return grouped
+            grouped_tiles[g] = grouped
 
-        def quantise(s, h, grouped):
-            codes, scales = quantised[s]
-            cols = slice(h * BANK, (h + 1) * BANK)
+        def quantise(g):
+            codes = mx_pool.tile([P, CHUNK], U32, name="codes", align_bytes=64)
+            scales = mx_pool.tile([P, CHUNK], U8, name="scales", align_bytes=64)
             nc.vector.quantize_mx(
-                out=codes[:, cols].bitcast(FP8X4),
-                scales=scales[:, cols],
-                in_=grouped[:, h * BANK * PACK : (h + 1) * BANK * PACK],
+                out=codes[:].bitcast(FP8X4), scales=scales[:], in_=grouped_tiles[g][:]
             )
+            quantised[g] = (codes, scales)
 
-        def multiply(s, h):
-            codes, scales = quantised[s]
-            cols = slice(h * BANK, (h + 1) * BANK)
-            start = s <= EDGES
-            stop = s < EDGES or s == N_STEPS - 1
+        def multiply(g):
+            codes, scales = quantised[g]
+            item, i = divmod(g, CHUNKS)
+            start = i <= EDGES
+            stop = i < EDGES or i == CHUNKS - 1
             if start:
-                k_open[h] = k_psum.tile([P, BANK], F32, name="k_acc")
+                k_open[item] = k_psum.tile([P, BANK], F32, name="k_acc")
             nc.tensor.matmul_mx(
-                out=k_open[h][:],
+                out=k_open[item][:],
                 lhsT=w_codes[:, 0:D_HEAD].bitcast(FP8X4),
                 lhsT_scale=w_scales[:, 0:D_HEAD],
-                rhs=codes[:, cols].bitcast(FP8X4),
-                rhs_scale=scales[:, cols],
+                rhs=codes[:].bitcast(FP8X4),
+                rhs_scale=scales[:],
                 start=start,
                 stop=stop,
             )
-            v_acc = v_psum.tile([P, TILES_PER_HALF, D_HEAD], F32, name="v_acc")
-            for i in range(TILES_PER_HALF):
-                tile_cols = slice(h * BANK + i * P, h * BANK + (i + 1) * P)
+            if i < EDGES:
+                nc.scalar.copy(out=k_edge[:, item, i, :], in_=k_open[item][:])
+            v_acc = v_psum.tile([P, TILES, D_HEAD], F32, name="v_acc")
+            for t in range(TILES):
+                cols = slice(t * P, (t + 1) * P)
                 nc.tensor.matmul_mx(
-                    out=v_acc[:, i, :],
-                    lhsT=codes[:, tile_cols].bitcast(FP8X4),
-                    lhsT_scale=scales[:, tile_cols],
+                    out=v_acc[:, t, :],
+                    lhsT=codes[:, cols].bitcast(FP8X4),
+                    lhsT_scale=scales[:, cols],
                     rhs=w_codes[:, D_HEAD : 2 * D_HEAD].bitcast(FP8X4),
                     rhs_scale=w_scales[:, D_HEAD : 2 * D_HEAD],
                     start=True,
@@ -133,37 +141,54 @@ def tile_localxlattention_pa_t_kernel(tc, kv, Wkv, k_ext, v):
                 )
             return v_acc
 
-        def copy_v_out(s, h, v_acc):
-            v_half = v_tiles[s][:, h * TILES_PER_HALF : (h + 1) * TILES_PER_HALF, :]
-            if h == 1 or s >= V_ON_SCALAR_FROM:
-                nc.scalar.copy(out=v_half, in_=v_acc[:])
+        def copy_v_out(g, v_acc, on_scalar):
+            v_rows = v_tiles[g // GROUP][:, g % GROUP, :]
+            v_flat = v_acc[:].rearrange("p t d -> p (t d)")
+            if on_scalar:
+                nc.scalar.copy(out=v_rows, in_=v_flat)
             else:
-                nc.vector.tensor_copy(out=v_half, in_=v_acc[:])
+                nc.vector.tensor_copy(out=v_rows, in_=v_flat)
 
-        def turn_k_back(j, h):
+        def sum_k(item):
+            inner = k_open[item][:]
+            first, last = k_edge[:, item, 0, :], k_edge[:, item, 1, :]
+            sums = [k_sumsT[:, item, j, :] for j in range(3)]
+            nc.vector.tensor_tensor(out=sums[ALL_BUT_LAST], in0=inner, in1=first, op=ADD)
+            nc.vector.tensor_tensor(out=sums[ALL_BUT_FIRST], in0=inner, in1=last, op=ADD)
+            nc.vector.tensor_tensor(out=sums[ALL], in0=sums[ALL_BUT_LAST], in1=last, op=ADD)
+
+        def turn_k_back(item, j, on_scalar):
             turned = turn_psum.tile([P, BANK], F32, name="turned")
-            for i in range(TILES_PER_HALF):
+            for t in range(TILES):
                 nc.tensor.transpose(
-                    turned[:, i * D_HEAD : (i + 1) * D_HEAD],
-                    k_sumsT[:, j, h, i * P : (i + 1) * P],
+                    turned[:, t * D_HEAD : (t + 1) * D_HEAD],
+                    k_sumsT[:, item, j, t * P : (t + 1) * P],
                     ident[:],
                 )
-            nc.scalar.copy(out=k_sums[:, j, h, :], in_=turned[:])
+            if on_scalar:
+                nc.scalar.copy(out=k_sums[:, item, j, :], in_=turned[:])
+            else:
+                nc.vector.tensor_copy(out=k_sums[:, item, j, :], in_=turned[:])
 
-        for s in range(KV_BUFS):
-            load(s, pieces=HALVES if s == 0 else 1)
+        def pieces_of(group):
+            return (EDGES, GROUP - EDGES) if group * GROUP % CHUNKS == 0 else (GROUP,)
+
+        load(0, (1, 1, GROUP - EDGES))
+        for group in range(1, KV_BUFS):
+            load(group, pieces_of(group))
 
         ident = const.tile([P, P], F32, name="ident")
         make_identity(nc, ident[:])
 
         w_rows = const.tile([P, PACK, 2 * D_HEAD], BF16, name="w_rows")
         nc.scalar.dma_start(out=w_rows[:], in_=Wkv.rearrange("(w j) n -> w j n", j=PACK))
-        k_edge = const.tile([P, EDGES, HALVES, BANK], F32, name="k_edge")
-        k_sumsT = const.tile([P, 3, HALVES, BANK], F32, name="k_sumsT")
-        k_sums = const.tile([P, 3, HALVES, BANK], F32, name="k_sums")
 
-        split_words(0)
-        load(KV_BUFS)
+        k_edge = const.tile([P, BATCH, EDGES, BANK], F32, name="k_edge")
+        k_sumsT = const.tile([P, BATCH, 3, BANK], F32, name="k_sumsT")
+        k_sums = const.tile([P, BATCH, 3, BANK], F32, name="k_sums")
+
+        for g in range(STEP):
+            split_words(g)
         w_grouped = const.tile([P, 2 * D_HEAD, PACK], BF16, name="w_grouped", align_bytes=64)
         nc.vector.tensor_copy(out=w_grouped[:], in_=w_rows[:].rearrange("w j n -> w n j"))
         w_codes = const.tile([P, 2 * D_HEAD], U32, name="w_codes", align_bytes=64)
@@ -174,54 +199,55 @@ def tile_localxlattention_pa_t_kernel(tc, kv, Wkv, k_ext, v):
             in_=w_grouped[:].rearrange("w n j -> w (n j)"),
         )
 
+        steps_of_item = CHUNKS // STEP
         for r in range(N_STEPS + 1):
             if r < N_STEPS:
-                grouped = transpose_and_regroup(r)
+                for g in range(r * STEP, (r + 1) * STEP):
+                    transpose_and_regroup(g)
+            bank_turn = r - steps_of_item - 1
+            if 0 <= bank_turn < len(BANKS_AS_SUMMED):
+                turn_k_back(0, BANKS_AS_SUMMED[bank_turn], on_scalar=True)
             if r + 1 < N_STEPS:
-                split_words(r + 1)
-                if r + 1 + KV_BUFS < N_STEPS:
-                    load(r + 1 + KV_BUFS)
+                for g in range((r + 1) * STEP, (r + 2) * STEP):
+                    split_words(g)
+                done, left = divmod((r + 2) * STEP, GROUP)
+                if left == 0 and done - 1 + KV_BUFS < N_GROUPS:
+                    load(done - 1 + KV_BUFS, pieces_of(done - 1 + KV_BUFS))
             if r >= 1:
-                v_tiles[r - 1] = v_pool.tile([P, TILES, D_HEAD], F32, name="v_sb")
-                v_accs = [multiply(r - 1, h) for h in range(HALVES)]
-            for h in range(HALVES):
+                if (r - 1) * STEP % GROUP == 0:
+                    v_tiles[(r - 1) * STEP // GROUP] = v_pool.tile(
+                        [P, GROUP, TILES * D_HEAD], F32, name="v_sb"
+                    )
+                v_accs = [multiply(g) for g in range((r - 1) * STEP, r * STEP)]
+            for h in range(STEP):
                 if r < N_STEPS:
-                    quantise(r, h, grouped)
+                    quantise(r * STEP + h)
                 if r >= 1:
-                    copy_v_out(r - 1, h, v_accs[h])
-            if 1 <= r <= EDGES:
-                for h in range(HALVES):
-                    nc.scalar.copy(out=k_edge[:, r - 1, h, :], in_=k_open[h][:])
+                    copy_v_out((r - 1) * STEP + h, v_accs[h], on_scalar=h == 1 or r == N_STEPS)
+            if r >= 1 and r % steps_of_item == 0:
+                sum_k(r // steps_of_item - 1)
 
-        for h in range(HALVES):
-            nc.vector.tensor_tensor(
-                out=k_sumsT[:, ALL_BUT_LAST, h, :], in0=k_open[h][:], in1=k_edge[:, 0, h, :], op=ADD
-            )
-        for h in range(HALVES):
-            nc.vector.tensor_tensor(
-                out=k_sumsT[:, ALL_BUT_FIRST, h, :], in0=k_open[h][:], in1=k_edge[:, 1, h, :], op=ADD
-            )
-        for h in range(HALVES):
-            nc.vector.tensor_tensor(
-                out=k_sumsT[:, ALL, h, :],
-                in0=k_sumsT[:, ALL_BUT_LAST, h, :],
-                in1=k_edge[:, 1, h, :],
-                op=ADD,
-            )
-        banks_as_summed = (ALL_BUT_LAST, ALL_BUT_FIRST, ALL)
-        for j in banks_as_summed:
-            for h in range(HALVES):
-                turn_k_back(j, h)
+        for j in BANKS_AS_SUMMED:
+            turn_k_back(1, j, on_scalar=j != ALL_BUT_FIRST)
 
-        for s in range(N_STEPS):
-            for b in range(BATCH):
+        def store_v(group, pieces):
+            at = 0
+            for n in pieces:
                 nc.sync.dma_start(
-                    out=chunk_rows(v, s, b),
-                    in_=v_tiles[s][b:P:BATCH, :, :].rearrange("q t d -> q (t d)"),
+                    out=chunk_rows(v, group * GROUP + at, n), in_=v_tiles[group][:, at : at + n, :]
                 )
-        for j in banks_as_summed:
-            for b in range(BATCH):
-                nc.sync.dma_start(
-                    out=k_ext[b, j].rearrange("(q t) d -> q (t d)", t=TILES),
-                    in_=k_sums[b:P:BATCH, j, :, :].rearrange("q h n -> q (h n)"),
-                )
+                at += n
+
+        def store_k(item, banks):
+            nc.sync.dma_start(
+                out=k_ext[item].rearrange("j (p t) d -> p j (t d)", t=TILES)[:, banks, :],
+                in_=k_sums[:, item, banks, :],
+            )
+
+        for group in range(N_GROUPS - 1):
+            store_v(group, pieces_of(group))
+            if group == N_GROUPS // 2:
+                store_k(0, slice(0, 3))
+        store_v(N_GROUPS - 1, (STEP, STEP))
+        for j in BANKS_AS_SUMMED:
+            store_k(1, slice(j, j + 1))

@@ -23,9 +23,10 @@ N_STEPS = TOTAL // STEP
 GROUP = 4
 N_GROUPS = TOTAL // GROUP
 KV_BUFS = N_GROUPS // 2
+SPLIT_TILES = TILES // 2
 BANK = 512
 ALL_BUT_LAST, ALL, ALL_BUT_FIRST = 0, 1, 2
-BANKS_AS_SUMMED = (ALL_BUT_LAST, ALL_BUT_FIRST, ALL)
+BANK_OF_EDGE = (ALL_BUT_LAST, ALL_BUT_FIRST)
 
 FLOPS = 2 * BATCH * LENGTH * D_MODEL * 2 * D_HEAD
 
@@ -64,38 +65,45 @@ def tile_localxlattention_pa_t_kernel(tc, kv, Wkv, k_ext, v):
             stride = chunk_of(g + 1) - first if n > 1 else 1
             return by_chunk[:, first : first + (n - 1) * stride + 1 : stride, :]
 
-        def load(group, pieces):
+        def load(group, pieces, halve_first=False):
             x = kv_pool.tile([P, GROUP, TILES * D_MODEL], BF16, name="x")
             at = 0
             for n in pieces:
-                nc.sync.dma_start(
-                    out=x[:, at : at + n, :], in_=chunk_rows(kv, group * GROUP + at, n)
-                )
+                rows = chunk_rows(kv, group * GROUP + at, n)
+                width = TILES * D_MODEL
+                cut = width // 2 if halve_first and at == 0 else 0
+                for cols in (slice(cut, width), slice(0, cut)) if cut else (slice(0, width),):
+                    nc.sync.dma_start(out=x[:, at : at + n, cols], in_=rows[:, :, cols])
                 at += n
             kv_tiles[group] = x
 
-        def split_words(g):
-            split = mx_pool.tile([P, TILES, 2, P], F32, name="split")
+        def words_of(g):
             words = kv_tiles[g // GROUP][:, g % GROUP, :].bitcast(F32)
+            return words.rearrange("p (t w u) -> p t w u", t=TILES, u=2)
+
+        def split_words(g):
+            split = mx_pool.tile([P, SPLIT_TILES, 2, P], F32, name="split")
             nc.vector.tensor_copy(
-                out=split[:], in_=words.rearrange("p (t w u) -> p t u w", t=TILES, u=2)
+                out=split[:], in_=words_of(g)[:, :SPLIT_TILES, :, :].rearrange("p t w u -> p t u w")
             )
             split_tiles[g] = split
 
-        def transpose_and_regroup(g):
+        def transpose_and_regroup(g, copy_on_vector=()):
             grouped = mx_pool.tile([P, CHUNK * PACK], BF16, name="grouped", align_bytes=64)
             grouped_words = grouped[:].bitcast(F32).rearrange("w (n u) -> w n u", u=2)
-            for first in range(0, TILES, PAIR):
+            for first in reversed(range(0, TILES, PAIR)):
                 turned = turn_psum.tile([P, BANK], F32, name="turned")
                 by_u = turned[:].rearrange("w (u n) -> w u n", u=2)
                 for i in range(PAIR):
+                    t = first + i
                     for u in range(2):
-                        nc.tensor.transpose(
-                            by_u[:, u, i * P : (i + 1) * P],
-                            split_tiles[g][:, first + i, u, :],
-                            ident[:],
-                        )
-                nc.scalar.copy(
+                        if t < SPLIT_TILES:
+                            rows = split_tiles[g][:, t, u, :]
+                        else:
+                            rows = words_of(g)[:, t, :, u]
+                        nc.tensor.transpose(by_u[:, u, i * P : (i + 1) * P], rows, ident[:])
+                copy = nc.vector.tensor_copy if first in copy_on_vector else nc.scalar.copy
+                copy(
                     out=grouped_words[:, first * P : (first + PAIR) * P, :],
                     in_=by_u.rearrange("w u n -> w n u"),
                 )
@@ -109,12 +117,30 @@ def tile_localxlattention_pa_t_kernel(tc, kv, Wkv, k_ext, v):
             )
             quantised[g] = (codes, scales)
 
-        def multiply(g):
+        def multiply_by_tile(g, out, half):
+            codes, scales = quantised[g]
+            w_cols = slice(half * D_HEAD, (half + 1) * D_HEAD)
+            for t in range(TILES):
+                cols = slice(t * P, (t + 1) * P)
+                nc.tensor.matmul_mx(
+                    out=out[:, t * D_HEAD : (t + 1) * D_HEAD],
+                    lhsT=codes[:, cols].bitcast(FP8X4),
+                    lhsT_scale=scales[:, cols],
+                    rhs=w_codes[:, w_cols].bitcast(FP8X4),
+                    rhs_scale=w_scales[:, w_cols],
+                    start=True,
+                    stop=True,
+                )
+
+        def multiply_k(g):
             codes, scales = quantised[g]
             item, i = divmod(g, CHUNKS)
-            start = i <= EDGES
-            stop = i < EDGES or i == CHUNKS - 1
-            if start:
+            if i < EDGES:
+                k_acc = k_psum.tile([P, BANK], F32, name="k_acc")
+                multiply_by_tile(g, k_acc, 0)
+                nc.scalar.copy(out=k_edge[:, item, BANK_OF_EDGE[i], :], in_=k_acc[:])
+                return
+            if i == EDGES:
                 k_open[item] = k_psum.tile([P, BANK], F32, name="k_acc")
             nc.tensor.matmul_mx(
                 out=k_open[item][:],
@@ -122,59 +148,45 @@ def tile_localxlattention_pa_t_kernel(tc, kv, Wkv, k_ext, v):
                 lhsT_scale=w_scales[:, 0:D_HEAD],
                 rhs=codes[:].bitcast(FP8X4),
                 rhs_scale=scales[:],
-                start=start,
-                stop=stop,
+                start=i == EDGES,
+                stop=i == CHUNKS - 1,
             )
-            if i < EDGES:
-                nc.scalar.copy(out=k_edge[:, item, i, :], in_=k_open[item][:])
-            v_acc = v_psum.tile([P, TILES, D_HEAD], F32, name="v_acc")
-            for t in range(TILES):
-                cols = slice(t * P, (t + 1) * P)
-                nc.tensor.matmul_mx(
-                    out=v_acc[:, t, :],
-                    lhsT=codes[:, cols].bitcast(FP8X4),
-                    lhsT_scale=scales[:, cols],
-                    rhs=w_codes[:, D_HEAD : 2 * D_HEAD].bitcast(FP8X4),
-                    rhs_scale=w_scales[:, D_HEAD : 2 * D_HEAD],
-                    start=True,
-                    stop=True,
-                )
+
+        def multiply_v(g):
+            v_acc = v_psum.tile([P, BANK], F32, name="v_acc")
+            multiply_by_tile(g, v_acc, 1)
             return v_acc
 
         def copy_v_out(g, v_acc, on_scalar):
             v_rows = v_tiles[g // GROUP][:, g % GROUP, :]
-            v_flat = v_acc[:].rearrange("p t d -> p (t d)")
-            if on_scalar:
-                nc.scalar.copy(out=v_rows, in_=v_flat)
-            else:
-                nc.vector.tensor_copy(out=v_rows, in_=v_flat)
+            copy = nc.scalar.copy if on_scalar else nc.vector.tensor_copy
+            copy(out=v_rows, in_=v_acc[:])
 
-        def sum_k(item):
-            inner = k_open[item][:]
-            first, last = k_edge[:, item, 0, :], k_edge[:, item, 1, :]
-            sums = [k_sumsT[:, item, j, :] for j in range(3)]
-            nc.vector.tensor_tensor(out=sums[ALL_BUT_LAST], in0=inner, in1=first, op=ADD)
-            nc.vector.tensor_tensor(out=sums[ALL_BUT_FIRST], in0=inner, in1=last, op=ADD)
-            nc.vector.tensor_tensor(out=sums[ALL], in0=sums[ALL_BUT_LAST], in1=last, op=ADD)
+        def empty_inner(item):
+            nc.scalar.copy(out=inner_T[:, item, :], in_=k_open[item][:])
 
-        def turn_k_back(item, j, on_scalar):
-            turned = turn_psum.tile([P, BANK], F32, name="turned")
+        def turn_inner(item):
+            turned = k_psum.tile([P, BANK], F32, name="k_acc")
             for t in range(TILES):
                 nc.tensor.transpose(
                     turned[:, t * D_HEAD : (t + 1) * D_HEAD],
-                    k_sumsT[:, item, j, t * P : (t + 1) * P],
+                    inner_T[:, item, t * P : (t + 1) * P],
                     ident[:],
                 )
-            if on_scalar:
-                nc.scalar.copy(out=k_sums[:, item, j, :], in_=turned[:])
-            else:
-                nc.vector.tensor_copy(out=k_sums[:, item, j, :], in_=turned[:])
+            return turned
+
+        def sum_k(item, turned):
+            for j in range(3):
+                nc.vector.tensor_tensor(
+                    out=k_sums[:, item, j, :], in0=turned[:], in1=k_edge[:, item, j, :], op=ADD
+                )
 
         def pieces_of(group):
             return (EDGES, GROUP - EDGES) if group * GROUP % CHUNKS == 0 else (GROUP,)
 
-        load(0, (1, 1, GROUP - EDGES))
-        for group in range(1, KV_BUFS):
+        load(0, (1,) * GROUP, halve_first=True)
+        load(1, (STEP, STEP))
+        for group in range(2, KV_BUFS):
             load(group, pieces_of(group))
 
         ident = const.tile([P, P], F32, name="ident")
@@ -183,8 +195,8 @@ def tile_localxlattention_pa_t_kernel(tc, kv, Wkv, k_ext, v):
         w_rows = const.tile([P, PACK, 2 * D_HEAD], BF16, name="w_rows")
         nc.scalar.dma_start(out=w_rows[:], in_=Wkv.rearrange("(w j) n -> w j n", j=PACK))
 
-        k_edge = const.tile([P, BATCH, EDGES, BANK], F32, name="k_edge")
-        k_sumsT = const.tile([P, BATCH, 3, BANK], F32, name="k_sumsT")
+        k_edge = const.tile([P, BATCH, 3, BANK], F32, name="k_edge")
+        inner_T = const.tile([P, BATCH, BANK], F32, name="inner_T")
         k_sums = const.tile([P, BATCH, 3, BANK], F32, name="k_sums")
 
         for g in range(STEP):
@@ -202,11 +214,11 @@ def tile_localxlattention_pa_t_kernel(tc, kv, Wkv, k_ext, v):
         steps_of_item = CHUNKS // STEP
         for r in range(N_STEPS + 1):
             if r < N_STEPS:
+                shared = (0,) if r == N_STEPS - 1 else ()
                 for g in range(r * STEP, (r + 1) * STEP):
-                    transpose_and_regroup(g)
-            bank_turn = r - steps_of_item - 1
-            if 0 <= bank_turn < len(BANKS_AS_SUMMED):
-                turn_k_back(0, BANKS_AS_SUMMED[bank_turn], on_scalar=True)
+                    transpose_and_regroup(g, copy_on_vector=shared)
+            if r == steps_of_item + EDGES:
+                first_turned = turn_inner(0)
             if r + 1 < N_STEPS:
                 for g in range((r + 1) * STEP, (r + 2) * STEP):
                     split_words(g)
@@ -218,17 +230,31 @@ def tile_localxlattention_pa_t_kernel(tc, kv, Wkv, k_ext, v):
                     v_tiles[(r - 1) * STEP // GROUP] = v_pool.tile(
                         [P, GROUP, TILES * D_HEAD], F32, name="v_sb"
                     )
-                v_accs = [multiply(g) for g in range((r - 1) * STEP, r * STEP)]
+                ready = range((r - 1) * STEP, r * STEP)
+                for g in ready:
+                    multiply_k(g)
+                if r == N_STEPS:
+                    empty_inner(1)
+                v_accs = [multiply_v(g) for g in ready]
             for h in range(STEP):
                 if r < N_STEPS:
                     quantise(r * STEP + h)
                 if r >= 1:
-                    copy_v_out((r - 1) * STEP + h, v_accs[h], on_scalar=h == 1 or r == N_STEPS)
-            if r >= 1 and r % steps_of_item == 0:
-                sum_k(r // steps_of_item - 1)
-
-        for j in BANKS_AS_SUMMED:
-            turn_k_back(1, j, on_scalar=j != ALL_BUT_FIRST)
+                    on_scalar = (h == 1 and r % 3 != 0) or r == N_STEPS - 1
+                    copy_v_out((r - 1) * STEP + h, v_accs[h], on_scalar)
+            if r == steps_of_item:
+                empty_inner(0)
+            if r == steps_of_item + EDGES:
+                sum_k(0, first_turned)
+            if r % steps_of_item == EDGES + 1:
+                item = r // steps_of_item
+                nc.vector.tensor_tensor(
+                    out=k_edge[:, item, ALL, :],
+                    in0=k_edge[:, item, ALL_BUT_LAST, :],
+                    in1=k_edge[:, item, ALL_BUT_FIRST, :],
+                    op=ADD,
+                )
+        sum_k(1, turn_inner(1))
 
         def store_v(group, pieces):
             at = 0
@@ -249,5 +275,5 @@ def tile_localxlattention_pa_t_kernel(tc, kv, Wkv, k_ext, v):
             if group == N_GROUPS // 2:
                 store_k(0, slice(0, 3))
         store_v(N_GROUPS - 1, (STEP, STEP))
-        for j in BANKS_AS_SUMMED:
+        for j in range(3):
             store_k(1, slice(j, j + 1))

@@ -23,7 +23,7 @@ N_STEPS = TOTAL // STEP
 GROUP = 4
 N_GROUPS = TOTAL // GROUP
 KV_BUFS = N_GROUPS // 2
-SPLIT_TILES = TILES // 2
+SPLIT_TILES = TILES - 1
 BANK = 512
 ALL_BUT_LAST, ALL, ALL_BUT_FIRST = 0, 1, 2
 BANK_OF_EDGE = (ALL_BUT_LAST, ALL_BUT_FIRST)
@@ -94,7 +94,7 @@ def tile_localxlattention_pa_t_kernel(tc, kv, Wkv, k_ext, v):
             for first in reversed(range(0, TILES, PAIR)):
                 turned = turn_psum.tile([P, BANK], F32, name="turned")
                 by_u = turned[:].rearrange("w (u n) -> w u n", u=2)
-                for i in range(PAIR):
+                for i in reversed(range(PAIR)):
                     t = first + i
                     for u in range(2):
                         if t < SPLIT_TILES:
@@ -240,7 +240,7 @@ def tile_localxlattention_pa_t_kernel(tc, kv, Wkv, k_ext, v):
                 if r < N_STEPS:
                     quantise(r * STEP + h)
                 if r >= 1:
-                    on_scalar = (h == 1 and r % 3 != 0) or r == N_STEPS - 1
+                    on_scalar = h == 1 or r == N_STEPS - 1
                     copy_v_out((r - 1) * STEP + h, v_accs[h], on_scalar)
             if r == steps_of_item:
                 empty_inner(0)

@@ -20,6 +20,7 @@ TILES = CHUNK // P
 PAIR = 2
 STEP = 2
 N_STEPS = TOTAL // STEP
+LAG = 2
 GROUP = 4
 N_GROUPS = TOTAL // GROUP
 KV_BUFS = N_GROUPS // 2
@@ -46,7 +47,7 @@ def tile_localxlattention_pa_t_kernel(tc, kv, Wkv, k_ext, v):
         ctx.enter_context(tc.manual_schedule())
         const = ctx.enter_context(tc.tile_pool(name="const", bufs=1))
         kv_pool = ctx.enter_context(tc.tile_pool(name="kv", bufs=KV_BUFS))
-        mx_pool = ctx.enter_context(tc.tile_pool(name="mx", bufs=2 * STEP))
+        mx_pool = ctx.enter_context(tc.tile_pool(name="mx", bufs=(LAG + 1) * STEP))
         v_pool = ctx.enter_context(tc.tile_pool(name="v", bufs=N_GROUPS))
         turn_psum = ctx.enter_context(tc.psum_pool(name="turn", bufs=4))
         v_psum = ctx.enter_context(tc.psum_pool(name="vp", bufs=STEP))
@@ -82,13 +83,13 @@ def tile_localxlattention_pa_t_kernel(tc, kv, Wkv, k_ext, v):
             return words.rearrange("p (t w u) -> p t w u", t=TILES, u=2)
 
         def split_words(g):
-            split = mx_pool.tile([P, SPLIT_TILES, 2, P], F32, name="split")
+            split = mx_pool.tile([P, 2, SPLIT_TILES, P], F32, name="split")
             nc.vector.tensor_copy(
-                out=split[:], in_=words_of(g)[:, :SPLIT_TILES, :, :].rearrange("p t w u -> p t u w")
+                out=split[:], in_=words_of(g)[:, :SPLIT_TILES, :, :].rearrange("p t w u -> p u t w")
             )
             split_tiles[g] = split
 
-        def transpose_and_regroup(g, copy_on_vector=()):
+        def transpose_and_regroup(g):
             grouped = mx_pool.tile([P, CHUNK * PACK], BF16, name="grouped", align_bytes=64)
             grouped_words = grouped[:].bitcast(F32).rearrange("w (n u) -> w n u", u=2)
             for first in reversed(range(0, TILES, PAIR)):
@@ -98,12 +99,11 @@ def tile_localxlattention_pa_t_kernel(tc, kv, Wkv, k_ext, v):
                     t = first + i
                     for u in range(2):
                         if t < SPLIT_TILES:
-                            rows = split_tiles[g][:, t, u, :]
+                            rows = split_tiles[g][:, u, t, :]
                         else:
                             rows = words_of(g)[:, t, :, u]
                         nc.tensor.transpose(by_u[:, u, i * P : (i + 1) * P], rows, ident[:])
-                copy = nc.vector.tensor_copy if first in copy_on_vector else nc.scalar.copy
-                copy(
+                nc.scalar.copy(
                     out=grouped_words[:, first * P : (first + PAIR) * P, :],
                     in_=by_u.rearrange("w u n -> w n u"),
                 )
@@ -181,13 +181,10 @@ def tile_localxlattention_pa_t_kernel(tc, kv, Wkv, k_ext, v):
                     out=k_sums[:, item, j, :], in0=turned[:], in1=k_edge[:, item, j, :], op=ADD
                 )
 
-        def pieces_of(group):
-            return (EDGES, GROUP - EDGES) if group * GROUP % CHUNKS == 0 else (GROUP,)
-
         load(0, (1,) * GROUP, halve_first=True)
-        load(1, (STEP, STEP))
+        load(1, (1,) * GROUP)
         for group in range(2, KV_BUFS):
-            load(group, pieces_of(group))
+            load(group, (STEP, STEP))
 
         ident = const.tile([P, P], F32, name="ident")
         make_identity(nc, ident[:])
@@ -210,44 +207,47 @@ def tile_localxlattention_pa_t_kernel(tc, kv, Wkv, k_ext, v):
             scales=w_scales[:],
             in_=w_grouped[:].rearrange("w n j -> w (n j)"),
         )
+        for g in range(STEP, LAG * STEP):
+            split_words(g)
+
+        def chunks_of(step):
+            return range(step * STEP, (step + 1) * STEP) if 0 <= step < N_STEPS else ()
 
         steps_of_item = CHUNKS // STEP
-        for r in range(N_STEPS + 1):
-            if r < N_STEPS:
-                shared = (0,) if r == N_STEPS - 1 else ()
-                for g in range(r * STEP, (r + 1) * STEP):
-                    transpose_and_regroup(g, copy_on_vector=shared)
-            if r == steps_of_item + EDGES:
+        for r in range(N_STEPS + LAG):
+            for g in chunks_of(r):
+                transpose_and_regroup(g)
+            left_group, rest = divmod((r + 1) * STEP, GROUP)
+            if rest == 0 and left_group - 1 + KV_BUFS < N_GROUPS:
+                load(left_group - 1 + KV_BUFS, (STEP, STEP))
+
+            ready = r - LAG
+            if ready == steps_of_item + 1:
                 first_turned = turn_inner(0)
-            if r + 1 < N_STEPS:
-                for g in range((r + 1) * STEP, (r + 2) * STEP):
-                    split_words(g)
-                done, left = divmod((r + 2) * STEP, GROUP)
-                if left == 0 and done - 1 + KV_BUFS < N_GROUPS:
-                    load(done - 1 + KV_BUFS, pieces_of(done - 1 + KV_BUFS))
-            if r >= 1:
-                if (r - 1) * STEP % GROUP == 0:
-                    v_tiles[(r - 1) * STEP // GROUP] = v_pool.tile(
-                        [P, GROUP, TILES * D_HEAD], F32, name="v_sb"
-                    )
-                ready = range((r - 1) * STEP, r * STEP)
-                for g in ready:
-                    multiply_k(g)
-                if r == N_STEPS:
-                    empty_inner(1)
-                v_accs = [multiply_v(g) for g in ready]
+            for g in chunks_of(ready):
+                multiply_k(g)
+            if ready == N_STEPS - 1:
+                empty_inner(1)
+            v_accs = [multiply_v(g) for g in chunks_of(ready)]
+
+            if ready >= 0 and ready * STEP % GROUP == 0:
+                v_tiles[ready * STEP // GROUP] = v_pool.tile(
+                    [P, GROUP, TILES * D_HEAD], F32, name="v_sb"
+                )
             for h in range(STEP):
+                if ready >= 0:
+                    copy_v_out(ready * STEP + h, v_accs[h], on_scalar=h == 1)
+                if r + LAG < N_STEPS:
+                    split_words((r + LAG) * STEP + h)
                 if r < N_STEPS:
                     quantise(r * STEP + h)
-                if r >= 1:
-                    on_scalar = h == 1 or r == N_STEPS - 1
-                    copy_v_out((r - 1) * STEP + h, v_accs[h], on_scalar)
-            if r == steps_of_item:
+
+            if ready == steps_of_item - 1:
                 empty_inner(0)
-            if r == steps_of_item + EDGES:
+            if ready == steps_of_item + 1:
                 sum_k(0, first_turned)
-            if r % steps_of_item == EDGES + 1:
-                item = r // steps_of_item
+            if ready >= 0 and ready % steps_of_item == 2:
+                item = ready // steps_of_item
                 nc.vector.tensor_tensor(
                     out=k_edge[:, item, ALL, :],
                     in0=k_edge[:, item, ALL_BUT_LAST, :],
@@ -271,7 +271,8 @@ def tile_localxlattention_pa_t_kernel(tc, kv, Wkv, k_ext, v):
             )
 
         for group in range(N_GROUPS - 1):
-            store_v(group, pieces_of(group))
+            first_of_item = group * GROUP % CHUNKS == 0
+            store_v(group, (EDGES, GROUP - EDGES) if first_of_item else (GROUP,))
             if group == N_GROUPS // 2:
                 store_k(0, slice(0, 3))
         store_v(N_GROUPS - 1, (STEP, STEP))

@@ -48,13 +48,12 @@ def tile_localxlattention_pa_t_kernel(tc, kv, Wkv, k_ext, v):
         const = ctx.enter_context(tc.tile_pool(name="const", bufs=1))
         kv_pool = ctx.enter_context(tc.tile_pool(name="kv", bufs=KV_BUFS))
         mx_pool = ctx.enter_context(tc.tile_pool(name="mx", bufs=(LAG + 1) * STEP))
-        v_pool = ctx.enter_context(tc.tile_pool(name="v", bufs=N_GROUPS))
+        v_pool = ctx.enter_context(tc.tile_pool(name="v", bufs=BATCH))
         turn_psum = ctx.enter_context(tc.psum_pool(name="turn", bufs=4))
         v_psum = ctx.enter_context(tc.psum_pool(name="vp", bufs=STEP))
         k_psum = ctx.enter_context(tc.psum_pool(name="kp", bufs=EDGES))
 
         kv_tiles = {}
-        v_tiles = {}
         split_tiles = {}
         grouped_tiles = {}
         quantised = {}
@@ -158,7 +157,7 @@ def tile_localxlattention_pa_t_kernel(tc, kv, Wkv, k_ext, v):
             return v_acc
 
         def copy_v_out(g, v_acc, on_scalar):
-            v_rows = v_tiles[g // GROUP][:, g % GROUP, :]
+            v_rows = v_tiles[item_of(g)][:, g % CHUNKS, :]
             copy = nc.scalar.copy if on_scalar else nc.vector.tensor_copy
             copy(out=v_rows, in_=v_acc[:])
 
@@ -180,6 +179,11 @@ def tile_localxlattention_pa_t_kernel(tc, kv, Wkv, k_ext, v):
                 nc.vector.tensor_tensor(
                     out=k_sums[:, item, j, :], in0=turned[:], in1=k_edge[:, item, j, :], op=ADD
                 )
+
+        v_tiles = []
+        for item in range(BATCH):
+            v_sb = v_pool.tile([P, CHUNKS, TILES * D_HEAD], F32, name="v_sb")
+            v_tiles.append(v_sb)
 
         load(0, (1,) * GROUP, halve_first=True)
         load(1, (1,) * GROUP)
@@ -219,7 +223,8 @@ def tile_localxlattention_pa_t_kernel(tc, kv, Wkv, k_ext, v):
                 transpose_and_regroup(g)
             left_group, rest = divmod((r + 1) * STEP, GROUP)
             if rest == 0 and left_group - 1 + KV_BUFS < N_GROUPS:
-                load(left_group - 1 + KV_BUFS, (STEP, STEP))
+                next_group = left_group - 1 + KV_BUFS
+                load(next_group, (STEP, STEP) if next_group == KV_BUFS else (GROUP,))
 
             ready = r - LAG
             if ready == steps_of_item + 1:
@@ -230,10 +235,6 @@ def tile_localxlattention_pa_t_kernel(tc, kv, Wkv, k_ext, v):
                 empty_inner(1)
             v_accs = [multiply_v(g) for g in chunks_of(ready)]
 
-            if ready >= 0 and ready * STEP % GROUP == 0:
-                v_tiles[ready * STEP // GROUP] = v_pool.tile(
-                    [P, GROUP, TILES * D_HEAD], F32, name="v_sb"
-                )
             for h in range(STEP):
                 if ready >= 0:
                     copy_v_out(ready * STEP + h, v_accs[h], on_scalar=h == 1)
@@ -256,11 +257,11 @@ def tile_localxlattention_pa_t_kernel(tc, kv, Wkv, k_ext, v):
                 )
         sum_k(1, turn_inner(1))
 
-        def store_v(group, pieces):
+        def store_v(item, pieces):
             at = 0
             for n in pieces:
                 nc.sync.dma_start(
-                    out=chunk_rows(v, group * GROUP + at, n), in_=v_tiles[group][:, at : at + n, :]
+                    out=chunk_rows(v, item * CHUNKS + at, n), in_=v_tiles[item][:, at : at + n, :]
                 )
                 at += n
 
@@ -270,11 +271,8 @@ def tile_localxlattention_pa_t_kernel(tc, kv, Wkv, k_ext, v):
                 in_=k_sums[:, item, banks, :],
             )
 
-        for group in range(N_GROUPS - 1):
-            first_of_item = group * GROUP % CHUNKS == 0
-            store_v(group, (EDGES, GROUP - EDGES) if first_of_item else (GROUP,))
-            if group == N_GROUPS // 2:
-                store_k(0, slice(0, 3))
-        store_v(N_GROUPS - 1, (STEP, STEP))
+        store_v(0, (EDGES, CHUNKS - EDGES))
+        store_k(0, slice(0, 3))
+        store_v(1, (EDGES, GROUP, GROUP, GROUP, STEP))
         for j in range(3):
             store_k(1, slice(j, j + 1))

@@ -32,6 +32,10 @@ BANK_OF_EDGE = (ALL_BUT_LAST, ALL_BUT_FIRST)
 FLOPS = 2 * BATCH * LENGTH * D_MODEL * 2 * D_HEAD
 
 
+def split_tiles_of(g):
+    return 0 if g == 0 else SPLIT_TILES
+
+
 def item_of(g):
     return g // CHUNKS
 
@@ -82,6 +86,8 @@ def tile_localxlattention_pa_t_kernel(tc, kv, Wkv, k_ext, v):
             return words.rearrange("p (t w u) -> p t w u", t=TILES, u=2)
 
         def split_words(g):
+            if split_tiles_of(g) == 0:
+                return
             split = mx_pool.tile([P, 2, SPLIT_TILES, P], F32, name="split")
             nc.vector.tensor_copy(
                 out=split[:], in_=words_of(g)[:, :SPLIT_TILES, :, :].rearrange("p t w u -> p u t w")
@@ -97,7 +103,7 @@ def tile_localxlattention_pa_t_kernel(tc, kv, Wkv, k_ext, v):
                 for i in reversed(range(PAIR)):
                     t = first + i
                     for u in range(2):
-                        if t < SPLIT_TILES:
+                        if t < split_tiles_of(g):
                             rows = split_tiles[g][:, u, t, :]
                         else:
                             rows = words_of(g)[:, t, :, u]
@@ -186,6 +192,10 @@ def tile_localxlattention_pa_t_kernel(tc, kv, Wkv, k_ext, v):
             v_tiles.append(v_sb)
 
         load(0, (1,) * GROUP, halve_first=True)
+
+        w_rows = const.tile([P, PACK, 2 * D_HEAD], BF16, name="w_rows")
+        nc.sync.dma_start(out=w_rows[:], in_=Wkv.rearrange("(w j) n -> w j n", j=PACK))
+
         load(1, (1,) * GROUP)
         for group in range(2, KV_BUFS):
             load(group, (STEP, STEP))
@@ -193,25 +203,23 @@ def tile_localxlattention_pa_t_kernel(tc, kv, Wkv, k_ext, v):
         ident = const.tile([P, P], F32, name="ident")
         make_identity(nc, ident[:])
 
-        w_rows = const.tile([P, PACK, 2 * D_HEAD], BF16, name="w_rows")
-        nc.scalar.dma_start(out=w_rows[:], in_=Wkv.rearrange("(w j) n -> w j n", j=PACK))
-
         k_edge = const.tile([P, BATCH, 3, BANK], F32, name="k_edge")
         inner_T = const.tile([P, BATCH, BANK], F32, name="inner_T")
         k_sums = const.tile([P, BATCH, 3, BANK], F32, name="k_sums")
 
-        for g in range(STEP):
-            split_words(g)
         w_grouped = const.tile([P, 2 * D_HEAD, PACK], BF16, name="w_grouped", align_bytes=64)
-        nc.vector.tensor_copy(out=w_grouped[:], in_=w_rows[:].rearrange("w j n -> w n j"))
         w_codes = const.tile([P, 2 * D_HEAD], U32, name="w_codes", align_bytes=64)
         w_scales = const.tile([P, 2 * D_HEAD], U8, name="w_scales", align_bytes=64)
-        nc.vector.quantize_mx(
-            out=w_codes[:].bitcast(FP8X4),
-            scales=w_scales[:],
-            in_=w_grouped[:].rearrange("w n j -> w (n j)"),
-        )
-        for g in range(STEP, LAG * STEP):
+
+        def quantise_w():
+            nc.vector.tensor_copy(out=w_grouped[:], in_=w_rows[:].rearrange("w j n -> w n j"))
+            nc.vector.quantize_mx(
+                out=w_codes[:].bitcast(FP8X4),
+                scales=w_scales[:],
+                in_=w_grouped[:].rearrange("w n j -> w (n j)"),
+            )
+
+        for g in range(LAG * STEP):
             split_words(g)
 
         def chunks_of(step):
@@ -242,6 +250,8 @@ def tile_localxlattention_pa_t_kernel(tc, kv, Wkv, k_ext, v):
                     split_words((r + LAG) * STEP + h)
                 if r < N_STEPS:
                     quantise(r * STEP + h)
+            if r == 0:
+                quantise_w()
 
             if ready == steps_of_item - 1:
                 empty_inner(0)
@@ -273,6 +283,6 @@ def tile_localxlattention_pa_t_kernel(tc, kv, Wkv, k_ext, v):
 
         store_v(0, (EDGES, CHUNKS - EDGES))
         store_k(0, slice(0, 3))
-        store_v(1, (EDGES, GROUP, GROUP, GROUP, STEP))
+        store_v(1, (EDGES, GROUP, GROUP, STEP, STEP, STEP))
         for j in range(3):
             store_k(1, slice(j, j + 1))

from contextlib import ExitStack

import concourse.mybir as mybir
from concourse.masks import make_identity

F32 = mybir.dt.float32
BF16 = mybir.dt.bfloat16
U32 = mybir.dt.uint32
U8 = mybir.dt.uint8
FP8X4 = mybir.dt.float8_e4m3fn_x4
ADD = mybir.AluOpType.add

P = 128
PACK = 4
BATCH, LENGTH, D_MODEL, D_HEAD, CHUNK = 2, 8192, 512, 128, 512
CHUNKS = LENGTH // CHUNK
TOTAL = BATCH * CHUNKS
EDGES = 2
TILES = CHUNK // P
PAIR = 2
STEP = 2
N_STEPS = TOTAL // STEP
LAG = 2
GROUP = 4
N_GROUPS = TOTAL // GROUP
KV_BUFS = N_GROUPS // 2
SPLIT_TILES = TILES - 1
BANK = 512
ALL_BUT_LAST, ALL, ALL_BUT_FIRST = 0, 1, 2
BANK_OF_EDGE = (ALL_BUT_LAST, ALL_BUT_FIRST)

FLOPS = 2 * BATCH * LENGTH * D_MODEL * 2 * D_HEAD


def split_tiles_of(g):
    return 0 if g == 0 else SPLIT_TILES


def item_of(g):
    return g // CHUNKS


def chunk_of(g):
    i = g % CHUNKS
    return (0, CHUNKS - 1)[i] if i < EDGES else i - 1


def tile_localxlattention_pa_t_kernel(tc, kv, Wkv, k_ext, v):
    nc = tc.nc
    with ExitStack() as ctx:
        ctx.enter_context(tc.manual_schedule())
        const = ctx.enter_context(tc.tile_pool(name="const", bufs=1))
        kv_pool = ctx.enter_context(tc.tile_pool(name="kv", bufs=KV_BUFS))
        mx_pool = ctx.enter_context(tc.tile_pool(name="mx", bufs=(LAG + 1) * STEP))
        v_pool = ctx.enter_context(tc.tile_pool(name="v", bufs=BATCH))
        turn_psum = ctx.enter_context(tc.psum_pool(name="turn", bufs=4))
        v_psum = ctx.enter_context(tc.psum_pool(name="vp", bufs=STEP))
        k_psum = ctx.enter_context(tc.psum_pool(name="kp", bufs=EDGES))

        kv_tiles = {}
        split_tiles = {}
        grouped_tiles = {}
        quantised = {}
        k_open = {}

        def chunk_rows(dram, g, n):
            by_chunk = dram[item_of(g)].rearrange("(c p t) d -> p c (t d)", p=P, t=TILES)
            first = chunk_of(g)
            stride = chunk_of(g + 1) - first if n > 1 else 1
            return by_chunk[:, first : first + (n - 1) * stride + 1 : stride, :]

        def load(group, pieces, halve_first=False):
            x = kv_pool.tile([P, GROUP, TILES * D_MODEL], BF16, name="x")
            at = 0
            for n in pieces:
                rows = chunk_rows(kv, group * GROUP + at, n)
                width = TILES * D_MODEL
                cut = width // 2 if halve_first and at == 0 else 0
                for cols in (slice(cut, width), slice(0, cut)) if cut else (slice(0, width),):
                    nc.sync.dma_start(out=x[:, at : at + n, cols], in_=rows[:, :, cols])
                at += n
            kv_tiles[group] = x

        def words_of(g):
            words = kv_tiles[g // GROUP][:, g % GROUP, :].bitcast(F32)
            return words.rearrange("p (t w u) -> p t w u", t=TILES, u=2)

        def split_words(g):
            if split_tiles_of(g) == 0:
                return
            split = mx_pool.tile([P, 2, SPLIT_TILES, P], F32, name="split")
            nc.vector.tensor_copy(
                out=split[:], in_=words_of(g)[:, :SPLIT_TILES, :, :].rearrange("p t w u -> p u t w")
            )
            split_tiles[g] = split

        def transpose_and_regroup(g):
            grouped = mx_pool.tile([P, CHUNK * PACK], BF16, name="grouped", align_bytes=64)
            grouped_words = grouped[:].bitcast(F32).rearrange("w (n u) -> w n u", u=2)
            for first in reversed(range(0, TILES, PAIR)):
                turned = turn_psum.tile([P, BANK], F32, name="turned")
                by_u = turned[:].rearrange("w (u n) -> w u n", u=2)
                for i in reversed(range(PAIR)):
                    t = first + i
                    for u in range(2):
                        if t < split_tiles_of(g):
                            rows = split_tiles[g][:, u, t, :]
                        else:
                            rows = words_of(g)[:, t, :, u]
                        nc.tensor.transpose(by_u[:, u, i * P : (i + 1) * P], rows, ident[:])
                nc.scalar.copy(
                    out=grouped_words[:, first * P : (first + PAIR) * P, :],
                    in_=by_u.rearrange("w u n -> w n u"),
                )
            grouped_tiles[g] = grouped

        def quantise(g):
            codes = mx_pool.tile([P, CHUNK], U32, name="codes", align_bytes=64)
            scales = mx_pool.tile([P, CHUNK], U8, name="scales", align_bytes=64)
            nc.vector.quantize_mx(
                out=codes[:].bitcast(FP8X4), scales=scales[:], in_=grouped_tiles[g][:]
            )
            quantised[g] = (codes, scales)

        def multiply_by_tile(g, out, half):
            codes, scales = quantised[g]
            w_cols = slice(half * D_HEAD, (half + 1) * D_HEAD)
            for t in range(TILES):
                cols = slice(t * P, (t + 1) * P)
                nc.tensor.matmul_mx(
                    out=out[:, t * D_HEAD : (t + 1) * D_HEAD],
                    lhsT=codes[:, cols].bitcast(FP8X4),
                    lhsT_scale=scales[:, cols],
                    rhs=w_codes[:, w_cols].bitcast(FP8X4),
                    rhs_scale=w_scales[:, w_cols],
                    start=True,
                    stop=True,
                )

        def multiply_k(g):
            codes, scales = quantised[g]
            item, i = divmod(g, CHUNKS)
            if i < EDGES:
                k_acc = k_psum.tile([P, BANK], F32, name="k_acc")
                multiply_by_tile(g, k_acc, 0)
                nc.scalar.copy(out=k_edge[:, item, BANK_OF_EDGE[i], :], in_=k_acc[:])
                return
            if i == EDGES:
                k_open[item] = k_psum.tile([P, BANK], F32, name="k_acc")
            nc.tensor.matmul_mx(
                out=k_open[item][:],
                lhsT=w_codes[:, 0:D_HEAD].bitcast(FP8X4),
                lhsT_scale=w_scales[:, 0:D_HEAD],
                rhs=codes[:].bitcast(FP8X4),
                rhs_scale=scales[:],
                start=i == EDGES,
                stop=i == CHUNKS - 1,
            )

        def multiply_v(g):
            v_acc = v_psum.tile([P, BANK], F32, name="v_acc")
            multiply_by_tile(g, v_acc, 1)
            return v_acc

        def copy_v_out(g, v_acc, on_scalar):
            v_rows = v_tiles[item_of(g)][:, g % CHUNKS, :]
            copy = nc.scalar.copy if on_scalar else nc.vector.tensor_copy
            copy(out=v_rows, in_=v_acc[:])

        def empty_inner(item):
            nc.scalar.copy(out=inner_T[:, item, :], in_=k_open[item][:])

        def turn_inner(item):
            turned = k_psum.tile([P, BANK], F32, name="k_acc")
            for t in range(TILES):
                nc.tensor.transpose(
                    turned[:, t * D_HEAD : (t + 1) * D_HEAD],
                    inner_T[:, item, t * P : (t + 1) * P],
                    ident[:],
                )
            return turned

        def sum_k(item, turned):
            for j in range(3):
                nc.vector.tensor_tensor(
                    out=k_sums[:, item, j, :], in0=turned[:], in1=k_edge[:, item, j, :], op=ADD
                )

        v_tiles = []
        for item in range(BATCH):
            v_sb = v_pool.tile([P, CHUNKS, TILES * D_HEAD], F32, name="v_sb")
            v_tiles.append(v_sb)

        load(0, (1,) * GROUP, halve_first=True)

        w_rows = const.tile([P, PACK, 2 * D_HEAD], BF16, name="w_rows")
        nc.sync.dma_start(out=w_rows[:], in_=Wkv.rearrange("(w j) n -> w j n", j=PACK))

        load(1, (1,) * GROUP)
        for group in range(2, KV_BUFS):
            load(group, (STEP, STEP))

        ident = const.tile([P, P], F32, name="ident")
        make_identity(nc, ident[:])

        k_edge = const.tile([P, BATCH, 3, BANK], F32, name="k_edge")
        inner_T = const.tile([P, BATCH, BANK], F32, name="inner_T")
        k_sums = const.tile([P, BATCH, 3, BANK], F32, name="k_sums")

        w_grouped = const.tile([P, 2 * D_HEAD, PACK], BF16, name="w_grouped", align_bytes=64)
        w_codes = const.tile([P, 2 * D_HEAD], U32, name="w_codes", align_bytes=64)
        w_scales = const.tile([P, 2 * D_HEAD], U8, name="w_scales", align_bytes=64)

        def quantise_w():
            nc.vector.tensor_copy(out=w_grouped[:], in_=w_rows[:].rearrange("w j n -> w n j"))
            nc.vector.quantize_mx(
                out=w_codes[:].bitcast(FP8X4),
                scales=w_scales[:],
                in_=w_grouped[:].rearrange("w n j -> w (n j)"),
            )

        for g in range(LAG * STEP):
            split_words(g)

        def chunks_of(step):
            return range(step * STEP, (step + 1) * STEP) if 0 <= step < N_STEPS else ()

        steps_of_item = CHUNKS // STEP
        for r in range(N_STEPS + LAG):
            for g in chunks_of(r):
                transpose_and_regroup(g)
            left_group, rest = divmod((r + 1) * STEP, GROUP)
            if rest == 0 and left_group - 1 + KV_BUFS < N_GROUPS:
                next_group = left_group - 1 + KV_BUFS
                load(next_group, (STEP, STEP) if next_group == KV_BUFS else (GROUP,))

            ready = r - LAG
            if ready == steps_of_item + 1:
                first_turned = turn_inner(0)
            for g in chunks_of(ready):
                multiply_k(g)
            if ready == N_STEPS - 1:
                empty_inner(1)
            v_accs = [multiply_v(g) for g in chunks_of(ready)]

            for h in range(STEP):
                if ready >= 0:
                    copy_v_out(ready * STEP + h, v_accs[h], on_scalar=h == 1)
                if r + LAG < N_STEPS:
                    split_words((r + LAG) * STEP + h)
                if r < N_STEPS:
                    quantise(r * STEP + h)
            if r == 0:
                quantise_w()

            if ready == steps_of_item - 1:
                empty_inner(0)
            if ready == steps_of_item + 1:
                sum_k(0, first_turned)
            if ready >= 0 and ready % steps_of_item == 2:
                item = ready // steps_of_item
                nc.vector.tensor_tensor(
                    out=k_edge[:, item, ALL, :],
                    in0=k_edge[:, item, ALL_BUT_LAST, :],
                    in1=k_edge[:, item, ALL_BUT_FIRST, :],
                    op=ADD,
                )
        sum_k(1, turn_inner(1))

        def store_v(item, pieces):
            at = 0
            for n in pieces:
                nc.sync.dma_start(
                    out=chunk_rows(v, item * CHUNKS + at, n), in_=v_tiles[item][:, at : at + n, :]
                )
                at += n

        def store_k(item, banks):
            nc.sync.dma_start(
                out=k_ext[item].rearrange("j (p t) d -> p j (t d)", t=TILES)[:, banks, :],
                in_=k_sums[:, item, banks, :],
            )

        store_v(0, (EDGES, CHUNKS - EDGES))
        store_k(0, slice(0, 3))
        store_v(1, (EDGES, GROUP, GROUP, STEP, STEP, STEP))
        for j in range(3):
            store_k(1, slice(j, j + 1))
